import numpy as np
import ml_dtypes

BF16 = ml_dtypes.bfloat16


def bf(x):
    return np.asarray(x, np.float32).astype(BF16)


def f32(x):
    return np.asarray(x, np.float32)


def f64(x):
    return np.asarray(x).astype(np.float64)


def striped(idx):
    return np.tile(idx.reshape(-1, 16).T, (8, 1))


S, D, M, N = 4096, 128, 512, 1024
EPS_BN = 1e-5


def mish(v):
    return v * np.tanh(np.log(1.0 + np.exp(v)))


def setup_inputs():
    return {"table": bf(np.random.standard_normal((S, D))), "w": bf(np.random.standard_normal((D, M)) / np.sqrt(D)), "b1": f32(0.2 * np.random.standard_normal((M, 1))), "gamma": f32(1.0 + 0.1 * np.random.standard_normal((M, 1))), "beta": f32(0.2 * np.random.standard_normal((M, 1))), "rmean": f32(0.2 * np.random.standard_normal((M, 1))), "rvar": f32(0.5 + np.random.random((M, 1))), "offs": striped(np.random.permutation(S)[:N])}


def reference(table, w, b1, gamma, beta, rmean, rvar, offs):
    idx = offs[:16].T.reshape(-1)
    h = f64(w).T @ f64(table)[idx].T + f64(b1)
    y = (h - f64(rmean)) / np.sqrt(f64(rvar) + EPS_BN) * f64(gamma) + f64(beta)
    return mish(y)

@@ -1,0 +1,126 @@
+import concourse.mybir as mybir
+from concourse.masks import make_identity
+
+S, D, M, N = 4096, 128, 512, 1024
+EPS_BN = 1e-5
+P = 128
+PIECE = 512
+PIECE_COLS = PIECE // 16
+N_PIECES = N // PIECE
+N_MB = M // P
+N_TILES = N_MB * N_PIECES
+CHUNK_ROWS = 1024
+BLOCKS_PER_CHUNK = CHUNK_ROWS // P
+FLIP_BLOCKS = 4
+LN_FLOOR = 2.0 ** -40
+
+FLOPS = 2 * D * M * N
+
+BF16, F32, U16 = mybir.dt.bfloat16, mybir.dt.float32, mybir.dt.uint16
+ALU = mybir.AluOpType
+ACT = mybir.ActivationFunctionType
+
+
+def tile_treedecoder_kernel(tc, table, w, b1, gamma, beta, rmean, rvar, offs, out):
+    nc = tc.nc
+    with (
+        tc.tile_pool(name="held", bufs=1) as held,
+        tc.tile_pool(name="results", bufs=3) as results,
+        tc.psum_pool(name="flips", bufs=2) as flips,
+        tc.psum_pool(name="spread", bufs=1) as spread,
+        tc.psum_pool(name="sums", bufs=4) as sums,
+    ):
+        offsets = held.tile([P, N // 16], U16, name="offsets")
+        nc.sync.dma_start(offsets[:], offs)
+
+        rows_of = held.tile([P, S // P, D], BF16, name="rows_of")
+        for c in range(S // CHUNK_ROWS):
+            queue = nc.sync if c % 2 == 0 else nc.scalar
+            queue.dma_start(
+                rows_of[:, c * BLOCKS_PER_CHUNK : (c + 1) * BLOCKS_PER_CHUNK, :],
+                table[c * CHUNK_ROWS : (c + 1) * CHUNK_ROWS, :].rearrange("(k p) d -> p k d", p=P),
+            )
+
+        weights = held.tile([D, M], BF16, name="weights")
+        nc.gpsimd.dma_start(weights[:], w)
+
+        vec_rows = held.tile([P, P], F32, name="vec_rows")
+        nc.vector.memset(vec_rows[:], 0.0)
+        for v, vec in enumerate((b1, gamma, beta, rmean, rvar)):
+            nc.gpsimd.dma_start(
+                vec_rows[v * N_MB : (v + 1) * N_MB, :],
+                vec.rearrange("(mb p) one -> mb (p one)", p=P),
+            )
+
+        ident_bf = held.tile([P, P], BF16, name="ident_bf")
+        make_identity(nc, ident_bf[:])
+        ident_f = held.tile([P, P], F32, name="ident_f")
+        make_identity(nc, ident_f[:])
+
+        vec_ps = spread.tile([P, P], F32, name="vec_ps")
+        nc.tensor.transpose(vec_ps[:], vec_rows[:], ident_f[:])
+        vecs = held.tile([P, 5 * N_MB], F32, name="vecs")
+        nc.vector.tensor_copy(vecs[:], vec_ps[:, 0 : 5 * N_MB])
+        b1_c, gamma_c, beta_c, rmean_c, rvar_c = (
+            vecs[:, v * N_MB : (v + 1) * N_MB] for v in range(5)
+        )
+
+        std = held.tile([P, N_MB], F32, name="std")
+        nc.vector.tensor_scalar_add(std[:], rvar_c, EPS_BN)
+        nc.scalar.sqrt(std[:], std[:])
+        scale = held.tile([P, N_MB], F32, name="scale")
+        nc.vector.reciprocal(scale[:], std[:])
+        nc.vector.tensor_mul(scale[:], scale[:], gamma_c)
+        shift = held.tile([P, N_MB], F32, name="shift")
+        nc.vector.tensor_sub(shift[:], b1_c, rmean_c)
+        nc.vector.tensor_mul(shift[:], shift[:], scale[:])
+        nc.vector.tensor_add(shift[:], shift[:], beta_c)
+
+        ln_floor = held.tile([P, 1], F32, name="ln_floor")
+        nc.vector.memset(ln_floor[:], LN_FLOOR)
+
+        window = held.tile([D, S], BF16, name="window")
+        for g in range(S // (FLIP_BLOCKS * P)):
+            flipped = flips.tile([D, FLIP_BLOCKS * P], BF16, name="flipped")
+            for j in range(FLIP_BLOCKS):
+                nc.tensor.transpose(
+                    flipped[:, j * P : (j + 1) * P], rows_of[:, g * FLIP_BLOCKS + j, :], ident_bf[:]
+                )
+            span = window[:, g * FLIP_BLOCKS * P : (g + 1) * FLIP_BLOCKS * P]
+            if g % 2 == 0:
+                nc.vector.tensor_copy(span, flipped[:])
+            else:
+                nc.scalar.copy(span, flipped[:])
+
+        y = held.tile([P, N_TILES * PIECE], F32, name="y")
+        sig = held.tile([P, N_TILES * PIECE], F32, name="sig")
+        ln_sig = held.tile([P, N_TILES * PIECE], F32, name="ln_sig")
+        gate = held.tile([P, N_TILES * PIECE], F32, name="gate")
+
+        for t in range(N_TILES):
+            mb, piece = divmod(t, N_PIECES)
+            cols = slice(t * PIECE, (t + 1) * PIECE)
+            acc = sums.tile([P, PIECE], F32, name="acc")
+            nc.tensor.matmul(
+                acc[:],
+                weights[:, mb * P : (mb + 1) * P],
+                window[:].indirect(offsets[:, piece * PIECE_COLS : (piece + 1) * PIECE_COLS]),
+                start=True,
+                stop=True,
+            )
+            nc.vector.tensor_scalar(
+                y[:, cols], acc[:], scale[:, mb : mb + 1], shift[:, mb : mb + 1], ALU.mult, ALU.add
+            )
+            nc.scalar.activation(sig[:, cols], y[:, cols], ACT.Sigmoid, scale=-1.0)
+
+        nc.scalar.activation(ln_sig[:], sig[:], ACT.Ln, bias=ln_floor[:, 0:1])
+
+        for t in range(N_TILES):
+            mb, piece = divmod(t, N_PIECES)
+            cols = slice(t * PIECE, (t + 1) * PIECE)
+            nc.scalar.activation(gate[:, cols], ln_sig[:, cols], ACT.Tanh, scale=-1.0)
+            result = results.tile([P, PIECE], F32, name="result")
+            nc.vector.tensor_mul(result[:], y[:, cols], gate[:, cols])
+            nc.sync.dma_start(
+                out[mb * P : (mb + 1) * P, piece * PIECE : (piece + 1) * PIECE], result[:]
+            )

@@ -25,38 +25,63 @@ def tile_treedecoder_kernel(tc, table, w, b1, gamma, beta, rmean, rvar, offs, ou
     nc = tc.nc
     with (
         tc.tile_pool(name="held", bufs=1) as held,
-        tc.tile_pool(name="results", bufs=3) as results,
-        tc.psum_pool(name="flips", bufs=2) as flips,
+        tc.psum_pool(name="flips", bufs=3) as flips,
         tc.psum_pool(name="spread", bufs=1) as spread,
         tc.psum_pool(name="sums", bufs=4) as sums,
     ):
-        offsets = held.tile([P, N // 16], U16, name="offsets")
-        nc.sync.dma_start(offsets[:], offs)
+        ident_bf = held.tile([P, P], BF16, name="ident_bf")
+        make_identity(nc, ident_bf[:])
 
         rows_of = held.tile([P, S // P, D], BF16, name="rows_of")
-        for c in range(S // CHUNK_ROWS):
-            queue = nc.sync if c % 2 == 0 else nc.scalar
+
+        def load_chunk(queue, c):
             queue.dma_start(
                 rows_of[:, c * BLOCKS_PER_CHUNK : (c + 1) * BLOCKS_PER_CHUNK, :],
                 table[c * CHUNK_ROWS : (c + 1) * CHUNK_ROWS, :].rearrange("(k p) d -> p k d", p=P),
             )
 
-        weights = held.tile([D, M], BF16, name="weights")
-        nc.gpsimd.dma_start(weights[:], w)
-
         vec_rows = held.tile([P, P], F32, name="vec_rows")
         nc.vector.memset(vec_rows[:], 0.0)
-        for v, vec in enumerate((b1, gamma, beta, rmean, rvar)):
-            nc.gpsimd.dma_start(
+
+        def load_vector(queue, v, vec):
+            queue.dma_start(
                 vec_rows[v * N_MB : (v + 1) * N_MB, :],
                 vec.rearrange("(mb p) one -> mb (p one)", p=P),
             )
 
-        ident_bf = held.tile([P, P], BF16, name="ident_bf")
-        make_identity(nc, ident_bf[:])
-        ident_f = held.tile([P, P], F32, name="ident_f")
-        make_identity(nc, ident_f[:])
+        offsets = held.tile([P, N // 16], U16, name="offsets")
+        weights = held.tile([D, M], BF16, name="weights")
 
+        load_chunk(nc.sync, 0)
+        load_chunk(nc.scalar, 1)
+        load_vector(nc.sync, 0, b1)
+        load_vector(nc.scalar, 1, gamma)
+        load_vector(nc.sync, 2, beta)
+        load_vector(nc.scalar, 3, rmean)
+        load_vector(nc.sync, 4, rvar)
+        load_chunk(nc.scalar, 2)
+        load_chunk(nc.sync, 3)
+        nc.sync.dma_start(offsets[:], offs)
+        nc.scalar.dma_start(weights[:], w)
+
+        window = held.tile([D, S], BF16, name="window")
+
+        def flip_chunk(c):
+            for g in range(c * BLOCKS_PER_CHUNK // FLIP_BLOCKS, (c + 1) * BLOCKS_PER_CHUNK // FLIP_BLOCKS):
+                flipped = flips.tile([D, FLIP_BLOCKS * P], BF16, name="flipped")
+                for j in range(FLIP_BLOCKS):
+                    nc.tensor.transpose(
+                        flipped[:, j * P : (j + 1) * P], rows_of[:, g * FLIP_BLOCKS + j, :], ident_bf[:]
+                    )
+                nc.vector.tensor_copy(
+                    window[:, g * FLIP_BLOCKS * P : (g + 1) * FLIP_BLOCKS * P], flipped[:]
+                )
+
+        flip_chunk(0)
+        flip_chunk(1)
+
+        ident_f = held.tile([P, P], F32, name="ident_f")
+        nc.vector.tensor_copy(ident_f[:], ident_bf[:])
         vec_ps = spread.tile([P, P], F32, name="vec_ps")
         nc.tensor.transpose(vec_ps[:], vec_rows[:], ident_f[:])
         vecs = held.tile([P, 5 * N_MB], F32, name="vecs")
@@ -65,37 +90,28 @@ def tile_treedecoder_kernel(tc, table, w, b1, gamma, beta, rmean, rvar, offs, ou
             vecs[:, v * N_MB : (v + 1) * N_MB] for v in range(5)
         )
 
-        std = held.tile([P, N_MB], F32, name="std")
-        nc.vector.tensor_scalar_add(std[:], rvar_c, EPS_BN)
-        nc.scalar.sqrt(std[:], std[:])
+        minus_half = held.tile([P, N_MB], F32, name="minus_half")
+        nc.gpsimd.memset(minus_half[:], -0.5)
         scale = held.tile([P, N_MB], F32, name="scale")
-        nc.vector.reciprocal(scale[:], std[:])
-        nc.vector.tensor_mul(scale[:], scale[:], gamma_c)
+        nc.gpsimd.tensor_scalar_add(scale[:], rvar_c, EPS_BN)
+        nc.gpsimd.tensor_tensor(scale[:], scale[:], minus_half[:], ALU.pow)
+        nc.gpsimd.tensor_mul(scale[:], scale[:], gamma_c)
         shift = held.tile([P, N_MB], F32, name="shift")
-        nc.vector.tensor_sub(shift[:], b1_c, rmean_c)
-        nc.vector.tensor_mul(shift[:], shift[:], scale[:])
-        nc.vector.tensor_add(shift[:], shift[:], beta_c)
+        nc.gpsimd.tensor_sub(shift[:], b1_c, rmean_c)
+        nc.gpsimd.tensor_mul(shift[:], shift[:], scale[:])
+        nc.gpsimd.tensor_add(shift[:], shift[:], beta_c)
 
         ln_floor = held.tile([P, 1], F32, name="ln_floor")
         nc.vector.memset(ln_floor[:], LN_FLOOR)
 
-        window = held.tile([D, S], BF16, name="window")
-        for g in range(S // (FLIP_BLOCKS * P)):
-            flipped = flips.tile([D, FLIP_BLOCKS * P], BF16, name="flipped")
-            for j in range(FLIP_BLOCKS):
-                nc.tensor.transpose(
-                    flipped[:, j * P : (j + 1) * P], rows_of[:, g * FLIP_BLOCKS + j, :], ident_bf[:]
-                )
-            span = window[:, g * FLIP_BLOCKS * P : (g + 1) * FLIP_BLOCKS * P]
-            if g % 2 == 0:
-                nc.vector.tensor_copy(span, flipped[:])
-            else:
-                nc.scalar.copy(span, flipped[:])
+        flip_chunk(2)
+        flip_chunk(3)
 
         y = held.tile([P, N_TILES * PIECE], F32, name="y")
         sig = held.tile([P, N_TILES * PIECE], F32, name="sig")
         ln_sig = held.tile([P, N_TILES * PIECE], F32, name="ln_sig")
         gate = held.tile([P, N_TILES * PIECE], F32, name="gate")
+        result = held.tile([P, N_TILES * PIECE], F32, name="result")
 
         for t in range(N_TILES):
             mb, piece = divmod(t, N_PIECES)
@@ -119,8 +135,7 @@ def tile_treedecoder_kernel(tc, table, w, b1, gamma, beta, rmean, rvar, offs, ou
             mb, piece = divmod(t, N_PIECES)
             cols = slice(t * PIECE, (t + 1) * PIECE)
             nc.scalar.activation(gate[:, cols], ln_sig[:, cols], ACT.Tanh, scale=-1.0)
-            result = results.tile([P, PIECE], F32, name="result")
-            nc.vector.tensor_mul(result[:], y[:, cols], gate[:, cols])
+            nc.vector.tensor_mul(result[:, cols], y[:, cols], gate[:, cols])
             nc.sync.dma_start(
-                out[mb * P : (mb + 1) * P, piece * PIECE : (piece + 1) * PIECE], result[:]
+                out[mb * P : (mb + 1) * P, piece * PIECE : (piece + 1) * PIECE], result[:, cols]
             )

@@ -33,52 +33,23 @@ def tile_treedecoder_kernel(tc, table, w, b1, gamma, beta, rmean, rvar, offs, ou
         make_identity(nc, ident_bf[:])
 
         rows_of = held.tile([P, S // P, D], BF16, name="rows_of")
-
-        def load_chunk(queue, c):
-            queue.dma_start(
+        for c in range(S // CHUNK_ROWS):
+            nc.sync.dma_start(
                 rows_of[:, c * BLOCKS_PER_CHUNK : (c + 1) * BLOCKS_PER_CHUNK, :],
                 table[c * CHUNK_ROWS : (c + 1) * CHUNK_ROWS, :].rearrange("(k p) d -> p k d", p=P),
             )
+        offsets = held.tile([P, N // 16], U16, name="offsets")
+        nc.sync.dma_start(offsets[:], offs)
 
         vec_rows = held.tile([P, P], F32, name="vec_rows")
         nc.vector.memset(vec_rows[:], 0.0)
-
-        def load_vector(queue, v, vec):
-            queue.dma_start(
+        for v, vec in enumerate((b1, gamma, beta, rmean, rvar)):
+            nc.scalar.dma_start(
                 vec_rows[v * N_MB : (v + 1) * N_MB, :],
                 vec.rearrange("(mb p) one -> mb (p one)", p=P),
             )
-
-        offsets = held.tile([P, N // 16], U16, name="offsets")
         weights = held.tile([D, M], BF16, name="weights")
-
-        load_chunk(nc.sync, 0)
-        load_chunk(nc.scalar, 1)
-        load_vector(nc.sync, 0, b1)
-        load_vector(nc.scalar, 1, gamma)
-        load_vector(nc.sync, 2, beta)
-        load_vector(nc.scalar, 3, rmean)
-        load_vector(nc.sync, 4, rvar)
-        load_chunk(nc.scalar, 2)
-        load_chunk(nc.sync, 3)
-        nc.sync.dma_start(offsets[:], offs)
         nc.scalar.dma_start(weights[:], w)
-
-        window = held.tile([D, S], BF16, name="window")
-
-        def flip_chunk(c):
-            for g in range(c * BLOCKS_PER_CHUNK // FLIP_BLOCKS, (c + 1) * BLOCKS_PER_CHUNK // FLIP_BLOCKS):
-                flipped = flips.tile([D, FLIP_BLOCKS * P], BF16, name="flipped")
-                for j in range(FLIP_BLOCKS):
-                    nc.tensor.transpose(
-                        flipped[:, j * P : (j + 1) * P], rows_of[:, g * FLIP_BLOCKS + j, :], ident_bf[:]
-                    )
-                nc.vector.tensor_copy(
-                    window[:, g * FLIP_BLOCKS * P : (g + 1) * FLIP_BLOCKS * P], flipped[:]
-                )
-
-        flip_chunk(0)
-        flip_chunk(1)
 
         ident_f = held.tile([P, P], F32, name="ident_f")
         nc.vector.tensor_copy(ident_f[:], ident_bf[:])
@@ -90,22 +61,30 @@ def tile_treedecoder_kernel(tc, table, w, b1, gamma, beta, rmean, rvar, offs, ou
             vecs[:, v * N_MB : (v + 1) * N_MB] for v in range(5)
         )
 
-        minus_half = held.tile([P, N_MB], F32, name="minus_half")
-        nc.gpsimd.memset(minus_half[:], -0.5)
-        scale = held.tile([P, N_MB], F32, name="scale")
-        nc.gpsimd.tensor_scalar_add(scale[:], rvar_c, EPS_BN)
-        nc.gpsimd.tensor_tensor(scale[:], scale[:], minus_half[:], ALU.pow)
-        nc.gpsimd.tensor_mul(scale[:], scale[:], gamma_c)
+        std = held.tile([P, N_MB], F32, name="std")
+        nc.vector.tensor_scalar_add(std[:], rvar_c, EPS_BN)
+        nc.scalar.sqrt(std[:], std[:])
         shift = held.tile([P, N_MB], F32, name="shift")
-        nc.gpsimd.tensor_sub(shift[:], b1_c, rmean_c)
-        nc.gpsimd.tensor_mul(shift[:], shift[:], scale[:])
-        nc.gpsimd.tensor_add(shift[:], shift[:], beta_c)
+        nc.vector.tensor_sub(shift[:], b1_c, rmean_c)
+        scale = held.tile([P, N_MB], F32, name="scale")
+        nc.vector.reciprocal(scale[:], std[:])
+        nc.vector.tensor_mul(scale[:], scale[:], gamma_c)
+        nc.vector.tensor_mul(shift[:], shift[:], scale[:])
+        nc.vector.tensor_add(shift[:], shift[:], beta_c)
 
         ln_floor = held.tile([P, 1], F32, name="ln_floor")
         nc.vector.memset(ln_floor[:], LN_FLOOR)
 
-        flip_chunk(2)
-        flip_chunk(3)
+        window = held.tile([D, S], BF16, name="window")
+        for g in range(S // (FLIP_BLOCKS * P)):
+            flipped = flips.tile([D, FLIP_BLOCKS * P], BF16, name="flipped")
+            for j in range(FLIP_BLOCKS):
+                nc.tensor.transpose(
+                    flipped[:, j * P : (j + 1) * P], rows_of[:, g * FLIP_BLOCKS + j, :], ident_bf[:]
+                )
+            nc.vector.tensor_copy(
+                window[:, g * FLIP_BLOCKS * P : (g + 1) * FLIP_BLOCKS * P], flipped[:]
+            )
 
         y = held.tile([P, N_TILES * PIECE], F32, name="y")
         sig = held.tile([P, N_TILES * PIECE], F32, name="sig")

@@ -9,9 +9,10 @@ PIECE_COLS = PIECE // 16
 N_PIECES = N // PIECE
 N_MB = M // P
 N_TILES = N_MB * N_PIECES
-CHUNK_ROWS = 1024
-BLOCKS_PER_CHUNK = CHUNK_ROWS // P
-FLIP_BLOCKS = 4
+GROUP_ROWS = 512
+ROWS_PER_PART = GROUP_ROWS // P
+N_GROUPS = S // GROUP_ROWS
+LOAD_GROUPS = 2
 LN_FLOOR = 2.0 ** -40
 
 FLOPS = 2 * D * M * N
@@ -33,23 +34,62 @@ def tile_treedecoder_kernel(tc, table, w, b1, gamma, beta, rmean, rvar, offs, ou
         make_identity(nc, ident_bf[:])
 
         rows_of = held.tile([P, S // P, D], BF16, name="rows_of")
-        for c in range(S // CHUNK_ROWS):
-            nc.sync.dma_start(
-                rows_of[:, c * BLOCKS_PER_CHUNK : (c + 1) * BLOCKS_PER_CHUNK, :],
-                table[c * CHUNK_ROWS : (c + 1) * CHUNK_ROWS, :].rearrange("(k p) d -> p k d", p=P),
+
+        def load_groups(queue, first):
+            queue.dma_start(
+                rows_of[:, first * ROWS_PER_PART : (first + LOAD_GROUPS) * ROWS_PER_PART, :].rearrange(
+                    "p (g k) d -> p g (k d)", g=LOAD_GROUPS
+                ),
+                table[first * GROUP_ROWS : (first + LOAD_GROUPS) * GROUP_ROWS, :].rearrange(
+                    "(g p k) d -> p g (k d)", g=LOAD_GROUPS, k=ROWS_PER_PART
+                ),
             )
-        offsets = held.tile([P, N // 16], U16, name="offsets")
-        nc.sync.dma_start(offsets[:], offs)
 
         vec_rows = held.tile([P, P], F32, name="vec_rows")
         nc.vector.memset(vec_rows[:], 0.0)
-        for v, vec in enumerate((b1, gamma, beta, rmean, rvar)):
-            nc.scalar.dma_start(
+
+        def load_vector(queue, v, vec):
+            queue.dma_start(
                 vec_rows[v * N_MB : (v + 1) * N_MB, :],
                 vec.rearrange("(mb p) one -> mb (p one)", p=P),
             )
+
+        offsets = held.tile([P, N // 16], U16, name="offsets")
         weights = held.tile([D, M], BF16, name="weights")
+
+        load_groups(nc.sync, 0)
+        load_groups(nc.scalar, 2)
+        load_groups(nc.sync, 4)
+        load_groups(nc.scalar, 6)
+        load_vector(nc.sync, 0, b1)
+        load_vector(nc.scalar, 1, gamma)
+        load_vector(nc.sync, 2, beta)
+        load_vector(nc.scalar, 3, rmean)
+        load_vector(nc.sync, 4, rvar)
         nc.scalar.dma_start(weights[:], w)
+        nc.sync.dma_start(offsets[:], offs)
+
+        ln_floor = held.tile([P, 1], F32, name="ln_floor")
+        nc.vector.memset(ln_floor[:], LN_FLOOR)
+        warm = held.tile([P, 1], F32, name="warm")
+        nc.scalar.activation(warm[:], ln_floor[:], ACT.Sigmoid)
+
+        window = held.tile([D, S], BF16, name="window")
+
+        def flip_group(g):
+            flipped = flips.tile([D, ROWS_PER_PART, P], BF16, name="flipped")
+            for k in range(ROWS_PER_PART):
+                nc.tensor.transpose(flipped[:, k, :], rows_of[:, g * ROWS_PER_PART + k, :], ident_bf[:])
+            copy_out = nc.scalar.copy if g % 2 == 0 else nc.vector.tensor_copy
+            copy_out(
+                window[:, g * GROUP_ROWS : (g + 1) * GROUP_ROWS].rearrange(
+                    "d (p k) -> d p k", k=ROWS_PER_PART
+                ),
+                flipped[:].rearrange("d k p -> d p k"),
+            )
+
+        for g in range(N_GROUPS // 2):
+            flip_group(g)
 
         ident_f = held.tile([P, P], F32, name="ident_f")
         nc.vector.tensor_copy(ident_f[:], ident_bf[:])
@@ -61,30 +101,20 @@ def tile_treedecoder_kernel(tc, table, w, b1, gamma, beta, rmean, rvar, offs, ou
             vecs[:, v * N_MB : (v + 1) * N_MB] for v in range(5)
         )
 
-        std = held.tile([P, N_MB], F32, name="std")
-        nc.vector.tensor_scalar_add(std[:], rvar_c, EPS_BN)
-        nc.scalar.sqrt(std[:], std[:])
+        minus_half = held.tile([P, N_MB], F32, name="minus_half")
+        nc.gpsimd.memset(minus_half[:], -0.5)
+        scale = held.tile([P, N_MB], F32, name="scale")
+        nc.vector.tensor_scalar_add(scale[:], rvar_c, EPS_BN)
+        nc.gpsimd.tensor_tensor(scale[:], scale[:], minus_half[:], ALU.pow)
         shift = held.tile([P, N_MB], F32, name="shift")
         nc.vector.tensor_sub(shift[:], b1_c, rmean_c)
-        scale = held.tile([P, N_MB], F32, name="scale")
-        nc.vector.reciprocal(scale[:], std[:])
+
+        for g in range(N_GROUPS // 2, N_GROUPS):
+            flip_group(g)
+
         nc.vector.tensor_mul(scale[:], scale[:], gamma_c)
         nc.vector.tensor_mul(shift[:], shift[:], scale[:])
         nc.vector.tensor_add(shift[:], shift[:], beta_c)
-
-        ln_floor = held.tile([P, 1], F32, name="ln_floor")
-        nc.vector.memset(ln_floor[:], LN_FLOOR)
-
-        window = held.tile([D, S], BF16, name="window")
-        for g in range(S // (FLIP_BLOCKS * P)):
-            flipped = flips.tile([D, FLIP_BLOCKS * P], BF16, name="flipped")
-            for j in range(FLIP_BLOCKS):
-                nc.tensor.transpose(
-                    flipped[:, j * P : (j + 1) * P], rows_of[:, g * FLIP_BLOCKS + j, :], ident_bf[:]
-                )
-            nc.vector.tensor_copy(
-                window[:, g * FLIP_BLOCKS * P : (g + 1) * FLIP_BLOCKS * P], flipped[:]
-            )
 
         y = held.tile([P, N_TILES * PIECE], F32, name="y")
         sig = held.tile([P, N_TILES * PIECE], F32, name="sig")

@@ -13,6 +13,7 @@ GROUP_ROWS = 512
 ROWS_PER_PART = GROUP_ROWS // P
 N_GROUPS = S // GROUP_ROWS
 LOAD_GROUPS = 2
+VEC_ROWS = 64
 LN_FLOOR = 2.0 ** -40
 
 FLOPS = 2 * D * M * N
@@ -24,12 +25,7 @@ ACT = mybir.ActivationFunctionType
 
 def tile_treedecoder_kernel(tc, table, w, b1, gamma, beta, rmean, rvar, offs, out):
     nc = tc.nc
-    with (
-        tc.tile_pool(name="held", bufs=1) as held,
-        tc.psum_pool(name="flips", bufs=3) as flips,
-        tc.psum_pool(name="spread", bufs=1) as spread,
-        tc.psum_pool(name="sums", bufs=4) as sums,
-    ):
+    with tc.tile_pool(name="held", bufs=1) as held:
         ident_bf = held.tile([P, P], BF16, name="ident_bf")
         make_identity(nc, ident_bf[:])
 
@@ -45,7 +41,7 @@ def tile_treedecoder_kernel(tc, table, w, b1, gamma, beta, rmean, rvar, offs, ou
                 ),
             )
 
-        vec_rows = held.tile([P, P], F32, name="vec_rows")
+        vec_rows = held.tile([VEC_ROWS, P], F32, name="vec_rows")
         nc.vector.memset(vec_rows[:], 0.0)
 
         def load_vector(queue, v, vec):
@@ -75,76 +71,96 @@ def tile_treedecoder_kernel(tc, table, w, b1, gamma, beta, rmean, rvar, offs, ou
         nc.scalar.activation(warm[:], ln_floor[:], ACT.Sigmoid)
 
         window = held.tile([D, S], BF16, name="window")
+        neg_scale = held.tile([P, N_MB], F32, name="neg_scale")
+        neg_shift = held.tile([P, N_MB], F32, name="neg_shift")
 
-        def flip_group(g):
-            flipped = flips.tile([D, ROWS_PER_PART, P], BF16, name="flipped")
-            for k in range(ROWS_PER_PART):
-                nc.tensor.transpose(flipped[:, k, :], rows_of[:, g * ROWS_PER_PART + k, :], ident_bf[:])
-            copy_out = nc.scalar.copy if g % 2 == 0 else nc.vector.tensor_copy
-            copy_out(
-                window[:, g * GROUP_ROWS : (g + 1) * GROUP_ROWS].rearrange(
-                    "d (p k) -> d p k", k=ROWS_PER_PART
-                ),
-                flipped[:].rearrange("d k p -> d p k"),
+        with (
+            tc.psum_pool(name="flips", bufs=4) as flips,
+            tc.psum_pool(name="spread", bufs=1) as spread,
+        ):
+            def flip_group(g):
+                flipped = flips.tile([D, ROWS_PER_PART, P], BF16, name="flipped")
+                for k in range(ROWS_PER_PART):
+                    nc.tensor.transpose(
+                        flipped[:, k, :], rows_of[:, g * ROWS_PER_PART + k, :], ident_bf[:]
+                    )
+                copy_out = nc.vector.tensor_copy if g % 2 == 0 else nc.scalar.copy
+                copy_out(
+                    window[:, g * GROUP_ROWS : (g + 1) * GROUP_ROWS].rearrange(
+                        "d (p k) -> d p k", k=ROWS_PER_PART
+                    ),
+                    flipped[:].rearrange("d k p -> d p k"),
+                )
+
+            for g in range(N_GROUPS):
+                flip_group(g)
+
+            ident_f = held.tile([VEC_ROWS, VEC_ROWS], F32, name="ident_f")
+            nc.vector.tensor_copy(ident_f[:], ident_bf[0:VEC_ROWS, 0:VEC_ROWS])
+            vec_ps = spread.tile([P, VEC_ROWS], F32, name="vec_ps")
+            nc.tensor.transpose(vec_ps[:], vec_rows[:], ident_f[:])
+            vecs = held.tile([P, 5 * N_MB], F32, name="vecs")
+            nc.vector.tensor_copy(vecs[:], vec_ps[:, 0 : 5 * N_MB])
+            b1_c, gamma_c, beta_c, rmean_c, rvar_c = (
+                vecs[:, v * N_MB : (v + 1) * N_MB] for v in range(5)
             )
 
-        for g in range(N_GROUPS // 2):
-            flip_group(g)
+            minus_half = held.tile([P, N_MB], F32, name="minus_half")
+            nc.gpsimd.memset(minus_half[:], -0.5)
+            rstd = held.tile([P, N_MB], F32, name="rstd")
+            nc.vector.tensor_scalar_add(rstd[:], rvar_c, EPS_BN)
+            nc.gpsimd.tensor_tensor(rstd[:], rstd[:], minus_half[:], ALU.pow)
 
-        ident_f = held.tile([P, P], F32, name="ident_f")
-        nc.vector.tensor_copy(ident_f[:], ident_bf[:])
-        vec_ps = spread.tile([P, P], F32, name="vec_ps")
-        nc.tensor.transpose(vec_ps[:], vec_rows[:], ident_f[:])
-        vecs = held.tile([P, 5 * N_MB], F32, name="vecs")
-        nc.vector.tensor_copy(vecs[:], vec_ps[:, 0 : 5 * N_MB])
-        b1_c, gamma_c, beta_c, rmean_c, rvar_c = (
-            vecs[:, v * N_MB : (v + 1) * N_MB] for v in range(5)
-        )
+            nc.vector.tensor_sub(neg_shift[:], b1_c, rmean_c)
+            nc.vector.scalar_tensor_tensor(neg_scale[:], rstd[:], -1.0, gamma_c, ALU.mult, ALU.mult)
+            nc.vector.tensor_mul(neg_shift[:], neg_shift[:], neg_scale[:])
+            nc.vector.tensor_sub(neg_shift[:], neg_shift[:], beta_c)
 
-        minus_half = held.tile([P, N_MB], F32, name="minus_half")
-        nc.gpsimd.memset(minus_half[:], -0.5)
-        scale = held.tile([P, N_MB], F32, name="scale")
-        nc.vector.tensor_scalar_add(scale[:], rvar_c, EPS_BN)
-        nc.gpsimd.tensor_tensor(scale[:], scale[:], minus_half[:], ALU.pow)
-        shift = held.tile([P, N_MB], F32, name="shift")
-        nc.vector.tensor_sub(shift[:], b1_c, rmean_c)
-
-        for g in range(N_GROUPS // 2, N_GROUPS):
-            flip_group(g)
-
-        nc.vector.tensor_mul(scale[:], scale[:], gamma_c)
-        nc.vector.tensor_mul(shift[:], shift[:], scale[:])
-        nc.vector.tensor_add(shift[:], shift[:], beta_c)
-
-        y = held.tile([P, N_TILES * PIECE], F32, name="y")
+        neg_y = held.tile([P, N_TILES * PIECE], F32, name="neg_y")
         sig = held.tile([P, N_TILES * PIECE], F32, name="sig")
         ln_sig = held.tile([P, N_TILES * PIECE], F32, name="ln_sig")
-        gate = held.tile([P, N_TILES * PIECE], F32, name="gate")
+        neg_gate = held.tile([P, N_TILES * PIECE], F32, name="neg_gate")
         result = held.tile([P, N_TILES * PIECE], F32, name="result")
 
-        for t in range(N_TILES):
-            mb, piece = divmod(t, N_PIECES)
-            cols = slice(t * PIECE, (t + 1) * PIECE)
-            acc = sums.tile([P, PIECE], F32, name="acc")
-            nc.tensor.matmul(
-                acc[:],
-                weights[:, mb * P : (mb + 1) * P],
-                window[:].indirect(offsets[:, piece * PIECE_COLS : (piece + 1) * PIECE_COLS]),
-                start=True,
-                stop=True,
-            )
-            nc.vector.tensor_scalar(
-                y[:, cols], acc[:], scale[:, mb : mb + 1], shift[:, mb : mb + 1], ALU.mult, ALU.add
-            )
-            nc.scalar.activation(sig[:, cols], y[:, cols], ACT.Sigmoid, scale=-1.0)
+        with tc.psum_pool(name="sums", bufs=N_TILES) as sums:
 
-        nc.scalar.activation(ln_sig[:], sig[:], ACT.Ln, bias=ln_floor[:, 0:1])
+            def gathered_matmul(t):
+                mb, piece = divmod(t, N_PIECES)
+                acc = sums.tile([P, PIECE], F32, name="acc")
+                nc.tensor.matmul(
+                    acc[:],
+                    weights[:, mb * P : (mb + 1) * P],
+                    window[:].indirect(offsets[:, piece * PIECE_COLS : (piece + 1) * PIECE_COLS]),
+                    start=True,
+                    stop=True,
+                )
+                return acc
 
-        for t in range(N_TILES):
-            mb, piece = divmod(t, N_PIECES)
-            cols = slice(t * PIECE, (t + 1) * PIECE)
-            nc.scalar.activation(gate[:, cols], ln_sig[:, cols], ACT.Tanh, scale=-1.0)
-            nc.vector.tensor_mul(result[:, cols], y[:, cols], gate[:, cols])
-            nc.sync.dma_start(
-                out[mb * P : (mb + 1) * P, piece * PIECE : (piece + 1) * PIECE], result[:, cols]
-            )
+            for t in range(N_TILES):
+                mb = t // N_PIECES
+                cols = slice(t * PIECE, (t + 1) * PIECE)
+                acc = gathered_matmul(t)
+                nc.scalar.activation(
+                    sig[:, cols], acc[:], ACT.Sigmoid,
+                    bias=neg_shift[:, mb : mb + 1], scale=neg_scale[:, mb : mb + 1],
+                )
+
+            nc.scalar.activation(ln_sig[:], sig[:], ACT.Ln, bias=ln_floor[:, 0:1])
+
+            for t in range(N_TILES):
+                mb = t // N_PIECES
+                cols = slice(t * PIECE, (t + 1) * PIECE)
+                acc = gathered_matmul(t)
+                nc.vector.tensor_scalar(
+                    neg_y[:, cols], acc[:],
+                    neg_scale[:, mb : mb + 1], neg_shift[:, mb : mb + 1], ALU.mult, ALU.add,
+                )
+
+            for t in range(N_TILES):
+                mb, piece = divmod(t, N_PIECES)
+                cols = slice(t * PIECE, (t + 1) * PIECE)
+                nc.scalar.activation(neg_gate[:, cols], ln_sig[:, cols], ACT.Tanh)
+                nc.vector.tensor_mul(result[:, cols], neg_y[:, cols], neg_gate[:, cols])
+                nc.sync.dma_start(
+                    out[mb * P : (mb + 1) * P, piece * PIECE : (piece + 1) * PIECE], result[:, cols]
+                )

@@ -92,7 +92,7 @@ def tile_treedecoder_kernel(tc, table, w, b1, gamma, beta, rmean, rvar, offs, ou
                     flipped[:].rearrange("d k p -> d p k"),
                 )
 
-            for g in range(N_GROUPS):
+            for g in range(N_GROUPS // 2):
                 flip_group(g)
 
             ident_f = held.tile([VEC_ROWS, VEC_ROWS], F32, name="ident_f")
@@ -110,8 +110,11 @@ def tile_treedecoder_kernel(tc, table, w, b1, gamma, beta, rmean, rvar, offs, ou
             rstd = held.tile([P, N_MB], F32, name="rstd")
             nc.vector.tensor_scalar_add(rstd[:], rvar_c, EPS_BN)
             nc.gpsimd.tensor_tensor(rstd[:], rstd[:], minus_half[:], ALU.pow)
-
             nc.vector.tensor_sub(neg_shift[:], b1_c, rmean_c)
+
+            for g in range(N_GROUPS // 2, N_GROUPS):
+                flip_group(g)
+
             nc.vector.scalar_tensor_tensor(neg_scale[:], rstd[:], -1.0, gamma_c, ALU.mult, ALU.mult)
             nc.vector.tensor_mul(neg_shift[:], neg_shift[:], neg_scale[:])
             nc.vector.tensor_sub(neg_shift[:], neg_shift[:], beta_c)

@@ -13,6 +13,7 @@ GROUP_ROWS = 512
 ROWS_PER_PART = GROUP_ROWS // P
 N_GROUPS = S // GROUP_ROWS
 LOAD_GROUPS = 2
+N_IDLE = 4
 VEC_ROWS = 64
 LN_FLOOR = 2.0 ** -40
 
@@ -78,6 +79,12 @@ def tile_treedecoder_kernel(tc, table, w, b1, gamma, beta, rmean, rvar, offs, ou
             tc.psum_pool(name="flips", bufs=4) as flips,
             tc.psum_pool(name="spread", bufs=1) as spread,
         ):
+            zeros = held.tile([P, PIECE], BF16, name="zeros")
+            nc.vector.memset(zeros[:], 0.0)
+            idle = spread.tile([P, PIECE], F32, name="idle")
+            for i in range(N_IDLE):
+                nc.tensor.matmul(idle[:], zeros[:, 0:P], zeros[:], start=True, stop=True)
+
             def flip_group(g):
                 flipped = flips.tile([D, ROWS_PER_PART, P], BF16, name="flipped")
                 for k in range(ROWS_PER_PART):

@@ -42,12 +42,14 @@ def tile_treedecoder_kernel(tc, table, w, b1, gamma, beta, rmean, rvar, offs, ou
                 ),
             )
 
+        var_rows = held.tile([VEC_ROWS, P], F32, name="var_rows")
+        nc.vector.memset(var_rows[:], 0.0)
         vec_rows = held.tile([VEC_ROWS, P], F32, name="vec_rows")
         nc.vector.memset(vec_rows[:], 0.0)
 
-        def load_vector(queue, v, vec):
+        def load_vector(queue, rows, v, vec):
             queue.dma_start(
-                vec_rows[v * N_MB : (v + 1) * N_MB, :],
+                rows[v * N_MB : (v + 1) * N_MB, :],
                 vec.rearrange("(mb p) one -> mb (p one)", p=P),
             )
 
@@ -56,15 +58,15 @@ def tile_treedecoder_kernel(tc, table, w, b1, gamma, beta, rmean, rvar, offs, ou
 
         load_groups(nc.sync, 0)
         load_groups(nc.scalar, 2)
-        load_groups(nc.sync, 4)
+        load_vector(nc.sync, var_rows, 0, rvar)
         load_groups(nc.scalar, 6)
-        load_vector(nc.sync, 0, b1)
-        load_vector(nc.scalar, 1, gamma)
-        load_vector(nc.sync, 2, beta)
-        load_vector(nc.scalar, 3, rmean)
-        load_vector(nc.sync, 4, rvar)
-        nc.scalar.dma_start(weights[:], w)
+        load_groups(nc.sync, 4)
+        load_vector(nc.scalar, vec_rows, 1, gamma)
+        load_vector(nc.sync, vec_rows, 0, b1)
+        load_vector(nc.scalar, vec_rows, 3, rmean)
+        load_vector(nc.sync, vec_rows, 2, beta)
         nc.sync.dma_start(offsets[:], offs)
+        nc.gpsimd.dma_start(weights[:], w)
 
         ln_floor = held.tile([P, 1], F32, name="ln_floor")
         nc.vector.memset(ln_floor[:], LN_FLOOR)
@@ -99,24 +101,26 @@ def tile_treedecoder_kernel(tc, table, w, b1, gamma, beta, rmean, rvar, offs, ou
                     flipped[:].rearrange("d k p -> d p k"),
                 )
 
+            ident_f = held.tile([VEC_ROWS, VEC_ROWS], F32, name="ident_f")
+            nc.vector.tensor_copy(ident_f[:], ident_bf[0:VEC_ROWS, 0:VEC_ROWS])
+            minus_half = held.tile([P, N_MB], F32, name="minus_half")
+            nc.gpsimd.memset(minus_half[:], -0.5)
+            var_ps = spread.tile([P, VEC_ROWS], F32, name="var_ps")
+            nc.tensor.transpose(var_ps[:], var_rows[:], ident_f[:])
+            rstd = held.tile([P, N_MB], F32, name="rstd")
+            nc.vector.tensor_scalar_add(rstd[:], var_ps[:, 0:N_MB], EPS_BN)
+            nc.gpsimd.tensor_tensor(rstd[:], rstd[:], minus_half[:], ALU.pow)
+
             for g in range(N_GROUPS // 2):
                 flip_group(g)
 
-            ident_f = held.tile([VEC_ROWS, VEC_ROWS], F32, name="ident_f")
-            nc.vector.tensor_copy(ident_f[:], ident_bf[0:VEC_ROWS, 0:VEC_ROWS])
             vec_ps = spread.tile([P, VEC_ROWS], F32, name="vec_ps")
             nc.tensor.transpose(vec_ps[:], vec_rows[:], ident_f[:])
-            vecs = held.tile([P, 5 * N_MB], F32, name="vecs")
-            nc.vector.tensor_copy(vecs[:], vec_ps[:, 0 : 5 * N_MB])
-            b1_c, gamma_c, beta_c, rmean_c, rvar_c = (
-                vecs[:, v * N_MB : (v + 1) * N_MB] for v in range(5)
+            vecs = held.tile([P, 4 * N_MB], F32, name="vecs")
+            nc.vector.tensor_copy(vecs[:], vec_ps[:, 0 : 4 * N_MB])
+            b1_c, gamma_c, beta_c, rmean_c = (
+                vecs[:, v * N_MB : (v + 1) * N_MB] for v in range(4)
             )
-
-            minus_half = held.tile([P, N_MB], F32, name="minus_half")
-            nc.gpsimd.memset(minus_half[:], -0.5)
-            rstd = held.tile([P, N_MB], F32, name="rstd")
-            nc.vector.tensor_scalar_add(rstd[:], rvar_c, EPS_BN)
-            nc.gpsimd.tensor_tensor(rstd[:], rstd[:], minus_half[:], ALU.pow)
             nc.vector.tensor_sub(neg_shift[:], b1_c, rmean_c)
 
             for g in range(N_GROUPS // 2, N_GROUPS):

@@ -16,6 +16,7 @@ LOAD_GROUPS = 2
 N_IDLE = 4
 VEC_ROWS = 64
 LN_FLOOR = 2.0 ** -40
+N_DIVIDED = 1
 
 FLOPS = 2 * D * M * N
 
@@ -159,22 +160,45 @@ def tile_treedecoder_kernel(tc, table, w, b1, gamma, beta, rmean, rvar, offs, ou
                     bias=neg_shift[:, mb : mb + 1], scale=neg_scale[:, mb : mb + 1],
                 )
 
-            nc.scalar.activation(ln_sig[:], sig[:], ACT.Ln, bias=ln_floor[:, 0:1])
+            through_scalar = slice(N_DIVIDED * PIECE, N_TILES * PIECE)
+            nc.scalar.activation(
+                ln_sig[:, through_scalar], sig[:, through_scalar], ACT.Ln, bias=ln_floor[:, 0:1]
+            )
 
-            for t in range(N_TILES):
+            def make_neg_y(t):
                 mb = t // N_PIECES
-                cols = slice(t * PIECE, (t + 1) * PIECE)
                 acc = gathered_matmul(t)
                 nc.vector.tensor_scalar(
-                    neg_y[:, cols], acc[:],
+                    neg_y[:, t * PIECE : (t + 1) * PIECE], acc[:],
                     neg_scale[:, mb : mb + 1], neg_shift[:, mb : mb + 1], ALU.mult, ALU.add,
                 )
 
-            for t in range(N_TILES):
+            def store(t):
                 mb, piece = divmod(t, N_PIECES)
+                nc.sync.dma_start(
+                    out[mb * P : (mb + 1) * P, piece * PIECE : (piece + 1) * PIECE],
+                    result[:, t * PIECE : (t + 1) * PIECE],
+                )
+
+            square = held.tile([P, N_DIVIDED * PIECE], F32, name="square")
+            divisor = held.tile([P, N_DIVIDED * PIECE], F32, name="divisor")
+            quotient = held.tile([P, N_DIVIDED * PIECE], F32, name="quotient")
+            for t in range(N_DIVIDED):
+                cols = slice(t * PIECE, (t + 1) * PIECE)
+                nc.vector.tensor_mul(square[:, cols], sig[:, cols], sig[:, cols])
+                nc.vector.tensor_scalar(divisor[:, cols], square[:, cols], -0.5, -0.5, ALU.mult, ALU.add)
+                nc.vector.reciprocal(quotient[:, cols], divisor[:, cols])
+                make_neg_y(t)
+                nc.vector.scalar_tensor_tensor(
+                    result[:, cols], quotient[:, cols], 1.0, neg_y[:, cols], ALU.add, ALU.mult
+                )
+                store(t)
+
+            for t in range(N_DIVIDED, N_TILES):
+                make_neg_y(t)
+
+            for t in range(N_DIVIDED, N_TILES):
                 cols = slice(t * PIECE, (t + 1) * PIECE)
                 nc.scalar.activation(neg_gate[:, cols], ln_sig[:, cols], ACT.Tanh)
                 nc.vector.tensor_mul(result[:, cols], neg_y[:, cols], neg_gate[:, cols])
-                nc.sync.dma_start(
-                    out[mb * P : (mb + 1) * P, piece * PIECE : (piece + 1) * PIECE], result[:, cols]
-                )
+                store(t)

@@ -57,15 +57,15 @@ def tile_treedecoder_kernel(tc, table, w, b1, gamma, beta, rmean, rvar, offs, ou
         offsets = held.tile([P, N // 16], U16, name="offsets")
         weights = held.tile([D, M], BF16, name="weights")
 
+        load_vector(nc.gpsimd, vec_rows, 2, beta)
         load_groups(nc.sync, 0)
         load_groups(nc.scalar, 2)
         load_vector(nc.sync, var_rows, 0, rvar)
-        load_groups(nc.scalar, 6)
-        load_groups(nc.sync, 4)
         load_vector(nc.scalar, vec_rows, 1, gamma)
         load_vector(nc.sync, vec_rows, 0, b1)
         load_vector(nc.scalar, vec_rows, 3, rmean)
-        load_vector(nc.sync, vec_rows, 2, beta)
+        load_groups(nc.sync, 4)
+        load_groups(nc.scalar, 6)
         nc.sync.dma_start(offsets[:], offs)
         nc.gpsimd.dma_start(weights[:], w)
 
@@ -112,9 +112,6 @@ def tile_treedecoder_kernel(tc, table, w, b1, gamma, beta, rmean, rvar, offs, ou
             nc.vector.tensor_scalar_add(rstd[:], var_ps[:, 0:N_MB], EPS_BN)
             nc.gpsimd.tensor_tensor(rstd[:], rstd[:], minus_half[:], ALU.pow)
 
-            for g in range(N_GROUPS // 2):
-                flip_group(g)
-
             vec_ps = spread.tile([P, VEC_ROWS], F32, name="vec_ps")
             nc.tensor.transpose(vec_ps[:], vec_rows[:], ident_f[:])
             vecs = held.tile([P, 4 * N_MB], F32, name="vecs")
@@ -123,13 +120,12 @@ def tile_treedecoder_kernel(tc, table, w, b1, gamma, beta, rmean, rvar, offs, ou
                 vecs[:, v * N_MB : (v + 1) * N_MB] for v in range(4)
             )
             nc.vector.tensor_sub(neg_shift[:], b1_c, rmean_c)
-
-            for g in range(N_GROUPS // 2, N_GROUPS):
-                flip_group(g)
-
             nc.vector.scalar_tensor_tensor(neg_scale[:], rstd[:], -1.0, gamma_c, ALU.mult, ALU.mult)
             nc.vector.tensor_mul(neg_shift[:], neg_shift[:], neg_scale[:])
             nc.vector.tensor_sub(neg_shift[:], neg_shift[:], beta_c)
+
+            for g in range(N_GROUPS):
+                flip_group(g)
 
         neg_y = held.tile([P, N_TILES * PIECE], F32, name="neg_y")
         sig = held.tile([P, N_TILES * PIECE], F32, name="sig")

import concourse.mybir as mybir
from concourse.masks import make_identity

S, D, M, N = 4096, 128, 512, 1024
EPS_BN = 1e-5
P = 128
PIECE = 512
PIECE_COLS = PIECE // 16
N_PIECES = N // PIECE
N_MB = M // P
N_TILES = N_MB * N_PIECES
GROUP_ROWS = 512
ROWS_PER_PART = GROUP_ROWS // P
N_GROUPS = S // GROUP_ROWS
LOAD_GROUPS = 2
N_IDLE = 4
VEC_ROWS = 64
LN_FLOOR = 2.0 ** -40
N_DIVIDED = 1

FLOPS = 2 * D * M * N

BF16, F32, U16 = mybir.dt.bfloat16, mybir.dt.float32, mybir.dt.uint16
ALU = mybir.AluOpType
ACT = mybir.ActivationFunctionType


def tile_treedecoder_kernel(tc, table, w, b1, gamma, beta, rmean, rvar, offs, out):
    nc = tc.nc
    with tc.tile_pool(name="held", bufs=1) as held:
        ident_bf = held.tile([P, P], BF16, name="ident_bf")
        make_identity(nc, ident_bf[:])

        rows_of = held.tile([P, S // P, D], BF16, name="rows_of")

        def load_groups(queue, first):
            queue.dma_start(
                rows_of[:, first * ROWS_PER_PART : (first + LOAD_GROUPS) * ROWS_PER_PART, :].rearrange(
                    "p (g k) d -> p g (k d)", g=LOAD_GROUPS
                ),
                table[first * GROUP_ROWS : (first + LOAD_GROUPS) * GROUP_ROWS, :].rearrange(
                    "(g p k) d -> p g (k d)", g=LOAD_GROUPS, k=ROWS_PER_PART
                ),
            )

        var_rows = held.tile([VEC_ROWS, P], F32, name="var_rows")
        nc.vector.memset(var_rows[:], 0.0)
        vec_rows = held.tile([VEC_ROWS, P], F32, name="vec_rows")
        nc.vector.memset(vec_rows[:], 0.0)

        def load_vector(queue, rows, v, vec):
            queue.dma_start(
                rows[v * N_MB : (v + 1) * N_MB, :],
                vec.rearrange("(mb p) one -> mb (p one)", p=P),
            )

        offsets = held.tile([P, N // 16], U16, name="offsets")
        weights = held.tile([D, M], BF16, name="weights")

        load_vector(nc.gpsimd, vec_rows, 2, beta)
        load_groups(nc.sync, 0)
        load_groups(nc.scalar, 2)
        load_vector(nc.sync, var_rows, 0, rvar)
        load_vector(nc.scalar, vec_rows, 1, gamma)
        load_vector(nc.sync, vec_rows, 0, b1)
        load_vector(nc.scalar, vec_rows, 3, rmean)
        load_groups(nc.sync, 4)
        load_groups(nc.scalar, 6)
        nc.sync.dma_start(offsets[:], offs)
        nc.gpsimd.dma_start(weights[:], w)

        ln_floor = held.tile([P, 1], F32, name="ln_floor")
        nc.vector.memset(ln_floor[:], LN_FLOOR)
        warm = held.tile([P, 1], F32, name="warm")
        nc.scalar.activation(warm[:], ln_floor[:], ACT.Sigmoid)

        window = held.tile([D, S], BF16, name="window")
        neg_scale = held.tile([P, N_MB], F32, name="neg_scale")
        neg_shift = held.tile([P, N_MB], F32, name="neg_shift")

        with (
            tc.psum_pool(name="flips", bufs=4) as flips,
            tc.psum_pool(name="spread", bufs=1) as spread,
        ):
            zeros = held.tile([P, PIECE], BF16, name="zeros")
            nc.vector.memset(zeros[:], 0.0)
            idle = spread.tile([P, PIECE], F32, name="idle")
            for i in range(N_IDLE):
                nc.tensor.matmul(idle[:], zeros[:, 0:P], zeros[:], start=True, stop=True)

            def flip_group(g):
                flipped = flips.tile([D, ROWS_PER_PART, P], BF16, name="flipped")
                for k in range(ROWS_PER_PART):
                    nc.tensor.transpose(
                        flipped[:, k, :], rows_of[:, g * ROWS_PER_PART + k, :], ident_bf[:]
                    )
                copy_out = nc.vector.tensor_copy if g % 2 == 0 else nc.scalar.copy
                copy_out(
                    window[:, g * GROUP_ROWS : (g + 1) * GROUP_ROWS].rearrange(
                        "d (p k) -> d p k", k=ROWS_PER_PART
                    ),
                    flipped[:].rearrange("d k p -> d p k"),
                )

            ident_f = held.tile([VEC_ROWS, VEC_ROWS], F32, name="ident_f")
            nc.vector.tensor_copy(ident_f[:], ident_bf[0:VEC_ROWS, 0:VEC_ROWS])
            minus_half = held.tile([P, N_MB], F32, name="minus_half")
            nc.gpsimd.memset(minus_half[:], -0.5)
            var_ps = spread.tile([P, VEC_ROWS], F32, name="var_ps")
            nc.tensor.transpose(var_ps[:], var_rows[:], ident_f[:])
            rstd = held.tile([P, N_MB], F32, name="rstd")
            nc.vector.tensor_scalar_add(rstd[:], var_ps[:, 0:N_MB], EPS_BN)
            nc.gpsimd.tensor_tensor(rstd[:], rstd[:], minus_half[:], ALU.pow)

            vec_ps = spread.tile([P, VEC_ROWS], F32, name="vec_ps")
            nc.tensor.transpose(vec_ps[:], vec_rows[:], ident_f[:])
            vecs = held.tile([P, 4 * N_MB], F32, name="vecs")
            nc.vector.tensor_copy(vecs[:], vec_ps[:, 0 : 4 * N_MB])
            b1_c, gamma_c, beta_c, rmean_c = (
                vecs[:, v * N_MB : (v + 1) * N_MB] for v in range(4)
            )
            nc.vector.tensor_sub(neg_shift[:], b1_c, rmean_c)
            nc.vector.scalar_tensor_tensor(neg_scale[:], rstd[:], -1.0, gamma_c, ALU.mult, ALU.mult)
            nc.vector.tensor_mul(neg_shift[:], neg_shift[:], neg_scale[:])
            nc.vector.tensor_sub(neg_shift[:], neg_shift[:], beta_c)

            for g in range(N_GROUPS):
                flip_group(g)

        neg_y = held.tile([P, N_TILES * PIECE], F32, name="neg_y")
        sig = held.tile([P, N_TILES * PIECE], F32, name="sig")
        ln_sig = held.tile([P, N_TILES * PIECE], F32, name="ln_sig")
        neg_gate = held.tile([P, N_TILES * PIECE], F32, name="neg_gate")
        result = held.tile([P, N_TILES * PIECE], F32, name="result")

        with tc.psum_pool(name="sums", bufs=N_TILES) as sums:

            def gathered_matmul(t):
                mb, piece = divmod(t, N_PIECES)
                acc = sums.tile([P, PIECE], F32, name="acc")
                nc.tensor.matmul(
                    acc[:],
                    weights[:, mb * P : (mb + 1) * P],
                    window[:].indirect(offsets[:, piece * PIECE_COLS : (piece + 1) * PIECE_COLS]),
                    start=True,
                    stop=True,
                )
                return acc

            for t in range(N_TILES):
                mb = t // N_PIECES
                cols = slice(t * PIECE, (t + 1) * PIECE)
                acc = gathered_matmul(t)
                nc.scalar.activation(
                    sig[:, cols], acc[:], ACT.Sigmoid,
                    bias=neg_shift[:, mb : mb + 1], scale=neg_scale[:, mb : mb + 1],
                )

            through_scalar = slice(N_DIVIDED * PIECE, N_TILES * PIECE)
            nc.scalar.activation(
                ln_sig[:, through_scalar], sig[:, through_scalar], ACT.Ln, bias=ln_floor[:, 0:1]
            )

            def make_neg_y(t):
                mb = t // N_PIECES
                acc = gathered_matmul(t)
                nc.vector.tensor_scalar(
                    neg_y[:, t * PIECE : (t + 1) * PIECE], acc[:],
                    neg_scale[:, mb : mb + 1], neg_shift[:, mb : mb + 1], ALU.mult, ALU.add,
                )

            def store(t):
                mb, piece = divmod(t, N_PIECES)
                nc.sync.dma_start(
                    out[mb * P : (mb + 1) * P, piece * PIECE : (piece + 1) * PIECE],
                    result[:, t * PIECE : (t + 1) * PIECE],
                )

            square = held.tile([P, N_DIVIDED * PIECE], F32, name="square")
            divisor = held.tile([P, N_DIVIDED * PIECE], F32, name="divisor")
            quotient = held.tile([P, N_DIVIDED * PIECE], F32, name="quotient")
            for t in range(N_DIVIDED):
                cols = slice(t * PIECE, (t + 1) * PIECE)
                nc.vector.tensor_mul(square[:, cols], sig[:, cols], sig[:, cols])
                nc.vector.tensor_scalar(divisor[:, cols], square[:, cols], -0.5, -0.5, ALU.mult, ALU.add)
                nc.vector.reciprocal(quotient[:, cols], divisor[:, cols])
                make_neg_y(t)
                nc.vector.scalar_tensor_tensor(
                    result[:, cols], quotient[:, cols], 1.0, neg_y[:, cols], ALU.add, ALU.mult
                )
                store(t)

            for t in range(N_DIVIDED, N_TILES):
                make_neg_y(t)

            for t in range(N_DIVIDED, N_TILES):
                cols = slice(t * PIECE, (t + 1) * PIECE)
                nc.scalar.activation(neg_gate[:, cols], ln_sig[:, cols], ACT.Tanh)
                nc.vector.tensor_mul(result[:, cols], neg_y[:, cols], neg_gate[:, cols])
                store(t)
